import numpy as np
import ml_dtypes


def mxq(x, axis, fmt="e4m3"):
    dtype, down = {"e4m3": (ml_dtypes.float8_e4m3fn, 7), "e5m2": (ml_dtypes.float8_e5m2, 14)}[fmt]
    v = np.moveaxis(np.asarray(x, np.float32).astype(ml_dtypes.bfloat16).astype(np.float64), axis, -1)
    blocks = v.reshape(v.shape[:-1] + (-1, 32))
    amax = np.abs(blocks).max(-1, keepdims=True)
    byte = np.maximum(np.where(amax > 0, np.frexp(amax)[1] - 1 + 127, 0) - down, 1)
    scale = np.exp2(byte - 127.0)
    codes = (blocks / scale).astype(np.float32).astype(dtype).astype(np.float64)
    return np.moveaxis((codes * scale).reshape(v.shape), -1, axis)


WIDE = False


def mx_kscale(k):
    if not WIDE:
        return np.ones(k)
    levels = np.array([10, -10, 5, -5, 0])
    if k % 512:
        return np.exp2(np.random.permutation(np.resize(levels, k // 32))).repeat(32)
    a = np.empty((k // 512, 16))
    for p in range(k // 512):
        a[p, :8] = np.random.permutation(np.resize(levels, 8))
        for g in range(8):
            far = levels[np.abs(levels - a[p, g]) >= 10]
            a[p, g + 8] = far[np.random.randint(len(far))]
    return np.exp2(a.ravel()).repeat(32)


BF16 = ml_dtypes.bfloat16


def bf(x):
    return np.asarray(x, np.float32).astype(BF16)


def f64(x):
    return np.asarray(x).astype(np.float64)


B, T, C, H, KV, HD = 2, 256, 2048, 16, 4, 128
NQ = H * HD
NK = KV * HD
HALF = HD // 2
ROPE_THETA = 10000.0


def apply_rope(u, cos, sin):
    ur = u.reshape(*u.shape[:-1], HALF, 2)
    ue, uo = ur[..., 0], ur[..., 1]
    c = cos[None, :, None, :]
    s = sin[None, :, None, :]
    out_e = ue * c - uo * s
    out_o = ue * s + uo * c
    return np.stack([out_e, out_o], axis=-1).reshape(u.shape)


def draw0():
    s = mx_kscale(C)
    inv_freq = 1.0 / ROPE_THETA ** (np.arange(0, HD, 2) / HD)
    angles = np.arange(T)[:, None] * inv_freq[None, :]
    return {"x": bf(np.random.standard_normal((B, T, C)) * s),
            "w_qkv": bf(np.random.standard_normal((NQ + NK + NK, C)) / np.sqrt(C) / s[None, :]),
            "freqs_cos": bf(np.cos(angles)),
            "freqs_sin": bf(np.sin(angles))}


def core(x, w_qkv, freqs_cos, freqs_sin):
    cos, sin = f64(freqs_cos), f64(freqs_sin)
    qkv = mxq(f64(x), 2, "e4m3") @ mxq(f64(w_qkv), 1, "e4m3").T
    q = qkv[..., :NQ].reshape(B, T, H, HD)
    k = qkv[..., NQ:NQ + NK].reshape(B, T, KV, HD)
    v = qkv[..., NQ + NK:].reshape(B, T, KV, HD)
    return apply_rope(q, cos, sin), apply_rope(k, cos, sin), v


def e4m3fn_bytes(y):
    return np.clip(np.asarray(y, np.float64), -448.0, 448.0).astype(np.float32).astype(ml_dtypes.float8_e4m3fn).view(np.uint8)


def e4m3fn_values(b):
    return np.asarray(b, np.uint8).view(ml_dtypes.float8_e4m3fn).astype(np.float64)


def setup_inputs():
    d = draw0()
    x0 = np.asarray(d['w_qkv']).astype(np.float64)
    s = (np.max(np.abs(x0), axis=(0,), keepdims=True) / 448.0).astype(np.float32)
    out = {}
    for k, v in d.items():
        if k == 'w_qkv':
            out['w_qkv_bytes'] = e4m3fn_bytes(x0 / s.astype(np.float64))
            out['w_qkv_scale'] = s
        else:
            out[k] = v
    return out


def reference(x, w_qkv_bytes, w_qkv_scale, freqs_cos, freqs_sin):
    return core(x, e4m3fn_values(w_qkv_bytes) * w_qkv_scale.astype(np.float64), freqs_cos, freqs_sin)

@@ -1,0 +1,399 @@
+from contextlib import ExitStack
+
+import concourse.mybir as mybir
+from concourse.masks import make_identity
+
+FLOPS = 2 * 512 * 2048 * 3072
+
+F32 = mybir.dt.float32
+BF16 = mybir.dt.bfloat16
+U32 = mybir.dt.uint32
+U8 = mybir.dt.uint8
+FP8 = mybir.dt.float8_e4m3fn
+FP8X4 = mybir.dt.float8_e4m3fn_x4
+COPY = mybir.ActivationFunctionType.Copy
+MULT = mybir.AluOpType.mult
+ADD = mybir.AluOpType.add
+
+P = 128
+UNITS = 24
+ROPE_BANKS = 20
+PE_LAG = 4
+PAIR_LAG = 3
+S_SLOT = {21: 18, 23: 21}
+S_UNITS = tuple(S_SLOT)
+
+
+def tile_causalselfattention_pa_kernel(
+    tc, x, w_qkv_bytes, w_qkv_scale, freqs_cos, freqs_sin, out_0, out_1, out_2
+):
+    nc = tc.nc
+    x_rows = x.flatten_outer_dims()
+    out_rows = [
+        out_0.rearrange("b t h d -> (b t) (h d)"),
+        out_1.rearrange("b t h d -> (b t) (h d)"),
+        out_2.rearrange("b t h d -> (b t) (h d)"),
+    ]
+
+    with ExitStack() as ctx:
+        const = ctx.enter_context(tc.tile_pool(name="const", bufs=1))
+        ring = ctx.enter_context(tc.tile_pool(name="ring", bufs=4))
+        psum = ctx.enter_context(tc.psum_pool(name="psum", bufs=4))
+        ctx.enter_context(tc.manual_schedule())
+
+        scale_sb = const.tile([P, 16], F32, name="scale_sb")
+        nc.scalar.dma_start(
+            out=scale_sb[:].rearrange("p (g t) -> p g t", t=4),
+            in_=w_qkv_scale.rearrange("o (g p t) -> p (o g) t", p=P, t=4),
+        )
+        cos_raw = const.tile([P, 2, 64], BF16, name="cos_raw")
+        nc.scalar.dma_start(out=cos_raw[:], in_=freqs_cos.rearrange("(th p) j -> p th j", p=P))
+        sin_raw = const.tile([P, 2, 64], BF16, name="sin_raw")
+        nc.scalar.dma_start(out=sin_raw[:], in_=freqs_sin.rearrange("(th p) j -> p th j", p=P))
+
+        warm_in = const.tile([P, 1], F32, name="warm_in")
+        warm_out = const.tile([P, 1], F32, name="warm_out")
+        nc.gpsimd.memset(warm_in[:], 0.0)
+        nc.scalar.copy(out=warm_out[:], in_=warm_in[:])
+
+        ident = const.tile([P, P], F32, name="ident")
+        make_identity(nc, ident[:])
+
+        wq = {}
+        wq0 = {}
+        xs = {}
+
+        def load_w0(h):
+            wq0[h] = const.tile([P, 2, 512], U8, name="wq0_%d" % h)
+            nc.sync.dma_start(
+                out=wq0[h][:], in_=w_qkv_bytes[256 * h : 256 * (h + 1), 0:512].rearrange("(a p) k -> p a k", p=P)
+            )
+
+        def load_w(j):
+            i, g = j // 4, j % 4
+            wq[j] = const.tile([P, 4, 512], U8, name="wq%d" % j)
+            nc.sync.dma_start(
+                out=wq[j][:],
+                in_=w_qkv_bytes[512 * i : 512 * (i + 1), 512 * g : 512 * (g + 1)].rearrange(
+                    "(a p) k -> p a k", p=P
+                ),
+            )
+
+        def load_x(m):
+            xs[m] = const.tile([P, 2048], BF16, name="xs%d" % m)
+            nc.sync.dma_start(out=xs[m][:], in_=x_rows[128 * m : 128 * (m + 1), :])
+
+        load_w0(0)
+        load_w0(1)
+        load_w(1)
+        load_w(2)
+        for m in range(4):
+            load_x(m)
+            load_w(m + 3)
+        for j in range(7, UNITS):
+            load_w(j)
+
+        cos2 = const.tile([P, 2, 64, 2], F32, name="cos2")
+        sin2 = const.tile([P, 2, 64, 2], F32, name="sin2")
+        sin_full = const.tile([P, 1024], F32, name="sin_full")
+        sign = const.tile([P, 2], F32, name="sign")
+
+        def tables():
+            nc.vector.memset(sign[:, 0:1], -1.0)
+            nc.vector.memset(sign[:, 1:2], 1.0)
+            nc.gpsimd.tensor_tensor(
+                out=sin2[:].rearrange("p t j e -> p (t j) e"),
+                in0=sin_raw[:].rearrange("p t j -> p (t j)").unsqueeze(2).to_broadcast([P, 128, 2]),
+                in1=sign[:].unsqueeze(1).to_broadcast([P, 128, 2]),
+                op=MULT,
+            )
+            nc.gpsimd.tensor_scalar(
+                out=cos2[:].rearrange("p t j e -> p (t j) e"),
+                in0=cos_raw[:].rearrange("p t j -> p (t j)").unsqueeze(2).to_broadcast([P, 128, 2]),
+                scalar1=1.0,
+                scalar2=0.0,
+                op0=MULT,
+                op1=ADD,
+            )
+            nc.gpsimd.tensor_scalar(
+                out=sin_full[:].rearrange("p (t h n) -> p t h n", t=2, h=4),
+                in0=sin2[:].rearrange("p t j e -> p t (j e)").unsqueeze(2).to_broadcast([P, 2, 4, 128]),
+                scalar1=1.0,
+                scalar2=0.0,
+                op0=MULT,
+                op1=ADD,
+            )
+
+        xg = [const.tile([P, 2048], BF16, name="xg%d" % m, align_bytes=64) for m in range(4)]
+        xc = [const.tile([P, 512], U32, name="xc%d" % m, align_bytes=64) for m in range(4)]
+        xsc = [const.tile([P, 512], U8, name="xsc%d" % m, align_bytes=64) for m in range(4)]
+
+        wb = {}
+        tp = {}
+        xt = {}
+        wg = {}
+        wc = {}
+        ws = {}
+        acc = {}
+        u_sb = {}
+        a_sb = {}
+        s_sb = {}
+        o_last = {}
+
+        def cast0():
+            wb[0] = ring.tile([P, 2048], BF16, name="wb", tag="wb", bufs=6)
+            for a in range(2):
+                nc.scalar.copy(out=wb[0][:, 512 * a : 512 * (a + 1)], in_=wq0[0][:, a, :].bitcast(FP8))
+            nc.vector.tensor_copy(out=wb[0][:, 1024:2048], in_=wq0[1][:].rearrange("p a k -> p (a k)").bitcast(FP8))
+
+        def cast1():
+            wb[1] = ring.tile([P, 2048], BF16, name="wb", tag="wb", bufs=6)
+            flat = wq[1][:].rearrange("p a k -> p (a k)")
+            nc.vector.tensor_copy(out=wb[1][:, 0:1024], in_=flat[:, 0:1024].bitcast(FP8))
+            nc.scalar.copy(out=wb[1][:, 1024:2048], in_=flat[:, 1024:2048].bitcast(FP8))
+
+        def cast(j):
+            wb[j] = ring.tile([P, 2048], BF16, name="wb", tag="wb", bufs=6)
+            nc.scalar.copy(out=wb[j][:], in_=wq[j][:].rearrange("p a k -> p (a k)").bitcast(FP8))
+
+        def turn(words, bank, h):
+            for a2 in range(2):
+                for u in range(2):
+                    a = 2 * h + a2
+                    nc.tensor.transpose(
+                        bank[:, u, 128 * a2 : 128 * (a2 + 1)],
+                        words[:, 256 * a + u : 256 * (a + 1) : 2],
+                        ident[:],
+                    )
+
+        def transposes(j, h):
+            tp[(j, h)] = psum.tile([P, 2, 256], F32, name="tp", tag="tp")
+            turn(wb[j][:].bitcast(F32), tp[(j, h)], h)
+
+        def transposes_by_u(j):
+            words = wb[j][:].bitcast(F32)
+            for u in range(2):
+                tp[(j, u)] = psum.tile([P, 2, 256], F32, name="tp", tag="tp")
+                for a in range(4):
+                    nc.tensor.transpose(
+                        tp[(j, u)][:].rearrange("p u r -> p (u r)")[:, 128 * a : 128 * (a + 1)],
+                        words[:, 256 * a + u : 256 * (a + 1) : 2],
+                        ident[:],
+                    )
+
+        def x_transposes(m, h):
+            words = xs[m][:].bitcast(F32)
+            xt[(m, h)] = psum.tile([P, 2, 2, 128], F32, name="xt", tag="acc")
+            for g2 in range(2):
+                g = 2 * h + g2
+                for u in range(2):
+                    nc.tensor.transpose(xt[(m, h)][:, g2, u, :], words[:, 256 * g + u : 256 * (g + 1) : 2], ident[:])
+
+        def x_out(m, h):
+            nc.scalar.copy(
+                out=xg[m][:, 1024 * h : 1024 * (h + 1)].bitcast(F32).rearrange("p (g r u) -> p g r u", g=2, u=2),
+                in_=xt[(m, h)][:].rearrange("p g u r -> p g r u"),
+            )
+
+        def x_quant(m):
+            nc.vector.quantize_mx(out=xc[m][:].bitcast(FP8X4), scales=xsc[m][:], in_=xg[m][:])
+
+        def scale_half(j, h):
+            g = j % 4
+            k, q = j // 2, j % 2
+            if k not in wg:
+                wg[k] = ring.tile([P, 4096], BF16, name="wg", tag="wg%d" % (k % 3), bufs=1, align_bytes=64)
+            c0 = 2048 * q + 1024 * h
+            nc.vector.tensor_tensor(
+                out=wg[k][:, c0 : c0 + 1024].rearrange("p (r u e) -> p r u e", u=2, e=2),
+                in0=tp[(j, h)][:]
+                .rearrange("p u r -> p (u r)")
+                .bitcast(BF16)
+                .rearrange("p (u r e) -> p r u e", u=2, e=2),
+                in1=scale_sb[:, 4 * g : 4 * g + 4]
+                .rearrange("p (o u e) -> p o u e", o=1, u=2, e=2)
+                .to_broadcast([P, 256, 2, 2]),
+                op=MULT,
+            )
+
+        def scale_on_scalar(j):
+            g = j % 4
+            k, q = j // 2, j % 2
+            if k not in wg:
+                wg[k] = ring.tile([P, 4096], BF16, name="wg", tag="wg%d" % (k % 3), bufs=1, align_bytes=64)
+            planes = ring.tile([P, 4, 512], BF16, name="planes", tag="planes", bufs=1)
+            for u in range(2):
+                bank = tp[(j, u)][:].rearrange("p u r -> p (u r)").bitcast(BF16).rearrange("p (r e) -> p e r", e=2)
+                for e in range(2):
+                    t = 2 * u + e
+                    nc.scalar.activation(
+                        out=planes[:, t, :], in_=bank[:, e, :], func=COPY, scale=scale_sb[:, 4 * g + t : 4 * g + t + 1]
+                    )
+            nc.scalar.copy(
+                out=wg[k][:, 2048 * q : 2048 * (q + 1)].rearrange("p (r t) -> p r t", t=4),
+                in_=planes[:].rearrange("p t r -> p r t"),
+            )
+
+        def quant(k):
+            wc[k] = ring.tile([P, 1024], U32, name="wc", tag="wc", bufs=4, align_bytes=64)
+            ws[k] = ring.tile([P, 1024], U8, name="ws", tag="ws", bufs=4, align_bytes=64)
+            nc.vector.quantize_mx(out=wc[k][:].bitcast(FP8X4), scales=ws[k][:], in_=wg[k][:])
+
+        def new_bank(b, tag):
+            acc[b] = psum.tile([P, 512], F32, name="acc", tag=tag)
+
+        def passes(b, gs):
+            i, m = b // 4, b % 4
+            for g in gs:
+                j = 4 * i + g
+                cols = slice(512 * (j % 2), 512 * (j % 2 + 1))
+                nc.tensor.matmul_mx(
+                    out=acc[b][:],
+                    lhsT=xc[m][:, 128 * g : 128 * (g + 1)].bitcast(FP8X4),
+                    lhsT_scale=xsc[m][:, 128 * g : 128 * (g + 1)],
+                    rhs=wc[j // 2][:, cols].bitcast(FP8X4),
+                    rhs_scale=ws[j // 2][:, cols],
+                    start=(g == 0),
+                    stop=(g == 3),
+                )
+
+        def out_view(b):
+            i = b // 4
+            dst = out_rows[0] if i < 4 else out_rows[i - 3]
+            c0 = 512 * i if i < 4 else 0
+            return dst[:, c0 : c0 + 512]
+
+        def store(b, tile_ap):
+            m = b % 4
+            nc.sync.dma_start(out=out_view(b)[128 * m : 128 * (m + 1), :], in_=tile_ap)
+
+        def store_pair(p, tile_ap):
+            m = (2 * p) % 4
+            nc.sync.dma_start(
+                out=out_view(2 * p)[128 * m : 128 * (m + 2), :].rearrange("(t p) c -> p t c", p=P),
+                in_=tile_ap.rearrange("p (t c) -> p t c", t=2),
+            )
+
+        def heads(ap):
+            return ap.rearrange("p (h j e) -> p h j e", h=4, e=2)
+
+        def pairs(ap):
+            return ap.rearrange("p (n e) -> p n e", e=2)
+
+        def table(t, b):
+            return t[:, b % 2, :, :].unsqueeze(1).to_broadcast([P, 4, 64, 2])
+
+        def half(t, b):
+            return t[:, 512 * (b % 2) : 512 * (b % 2 + 1)]
+
+        def copy_u(b):
+            if b % 2 == 0:
+                u_sb[b // 2] = ring.tile([P, 1024], F32, name="u_sb", tag="u_sb", bufs=3)
+            nc.scalar.copy(out=half(u_sb[b // 2], b), in_=acc[b][:])
+
+        def rope_cos(b):
+            if b % 2 == 0:
+                a_sb[b // 2] = ring.tile([P, 1024], F32, name="a_sb", tag="a_sb", bufs=3)
+            nc.vector.tensor_tensor(out=heads(half(a_sb[b // 2], b)), in0=heads(acc[b][:]), in1=table(cos2, b), op=MULT)
+
+        def rope_sin(p, k):
+            s_sb[p] = ring.tile([P, 1024], F32, name="s_sb", tag="wg%d" % ((k - 1) % 3), bufs=1, align_bytes=64)
+            nc.gpsimd.tensor_tensor(
+                out=pairs(s_sb[p][:]), in0=pairs(u_sb[p][:])[:, :, ::-1], in1=pairs(sin_full[:]), op=MULT
+            )
+
+        def rope_add(p, eng):
+            o_sb = ring.tile([P, 1024], F32, name="o_sb", tag="o_sb", bufs=4)
+            eng.tensor_tensor(out=o_sb[:], in0=a_sb[p][:], in1=s_sb[p][:], op=ADD)
+            store_pair(p, o_sb[:])
+
+        def rope_sin_on_vector(p):
+            s_sb[p] = ring.tile([P, 1024], F32, name="s_v", tag="s_v", bufs=1)
+            for b in (2 * p, 2 * p + 1):
+                nc.vector.tensor_tensor(
+                    out=heads(half(s_sb[p], b)), in0=heads(acc[b][:])[:, :, :, ::-1], in1=table(sin2, b), op=MULT
+                )
+            o_last[p] = ring.tile([P, 1024], F32, name="o_sb", tag="o_sb", bufs=4)
+
+        def rope_add_bank(b):
+            p = b // 2
+            nc.vector.tensor_tensor(out=half(o_last[p], b), in0=half(a_sb[p], b), in1=half(s_sb[p], b), op=ADD)
+            store(b, half(o_last[p], b))
+
+        def plain_out(b):
+            v_sb = ring.tile([P, 512], F32, name="v_sb", tag="v_sb", bufs=4)
+            nc.scalar.copy(out=v_sb[:], in_=acc[b][:])
+            store(b, v_sb[:])
+
+        cast0()
+        cast1()
+        tables()
+        transposes(0, 0)
+        transposes(0, 1)
+        for s in range(UNITS):
+            k = s // 2
+            b = s - PE_LAG
+            p = k - PAIR_LAG
+            if s % 2 == 0:
+                scale_half(s, 0)
+                if 3 <= s <= 6:
+                    x_quant(s - 3)
+                if s - 1 in S_UNITS:
+                    rope_add(p - 1, nc.vector)
+                if k >= 1:
+                    quant(k - 1)
+                if p >= 0:
+                    rope_cos(2 * p)
+                    rope_sin(p, k)
+                scale_half(s, 1)
+            else:
+                if p >= 0:
+                    rope_cos(2 * p + 1)
+                if s not in S_UNITS:
+                    if p >= 0:
+                        rope_add(p, nc.gpsimd)
+                    scale_half(s, 0)
+                    if 3 <= s <= 6:
+                        x_quant(s - 3)
+                    scale_half(s, 1)
+            x_banks = [(m, h) for m in range(4) for h in range(2) if m + 1 + h == s]
+            for m, h in x_banks:
+                x_transposes(m, h)
+            if b >= 0:
+                new_bank(b, "acc")
+            for h in range(2):
+                if s + 1 < UNITS and s + 1 not in S_UNITS:
+                    transposes(s + 1, h)
+                if b >= 0:
+                    passes(b, (2 * h, 2 * h + 1))
+            early = [j for j in S_UNITS if S_SLOT[j] == s]
+            for j in early:
+                transposes_by_u(j)
+            if s >= UNITS - 2:
+                for m in (2 * (s % 2), 2 * (s % 2) + 1):
+                    new_bank(ROPE_BANKS + m, "acc" if m < 2 else "tp")
+                    passes(ROPE_BANKS + m, (0, 1))
+            for m, h in x_banks:
+                x_out(m, h)
+            lead = 2 if s < 4 else (3 if s < 8 else (4 if s < 12 else 5))
+            for j in range(UNITS):
+                if j not in wb and (j <= s + lead or (j in S_UNITS and S_SLOT[j] == s + 1)):
+                    cast(j)
+            if 0 <= b < ROPE_BANKS - 2:
+                copy_u(b)
+            for j in early:
+                scale_on_scalar(j)
+        last = ROPE_BANKS // 2 - 1
+        rope_cos(2 * last)
+        rope_add(last - 1, nc.vector)
+        quant(UNITS // 2 - 1)
+        for m in range(4):
+            passes(ROPE_BANKS + m, (2, 3))
+        rope_cos(2 * last + 1)
+        rope_sin_on_vector(last)
+        plain_out(ROPE_BANKS)
+        plain_out(ROPE_BANKS + 1)
+        rope_add_bank(2 * last)
+        plain_out(ROPE_BANKS + 2)
+        rope_add_bank(2 * last + 1)
+        plain_out(ROPE_BANKS + 3)

@@ -230,8 +230,8 @@ def tile_causalselfattention_pa_kernel(
                         out=planes[:, t, :], in_=bank[:, e, :], func=COPY, scale=scale_sb[:, 4 * g + t : 4 * g + t + 1]
                     )
             nc.scalar.copy(
-                out=wg[k][:, 2048 * q : 2048 * (q + 1)].rearrange("p (r t) -> p r t", t=4),
-                in_=planes[:].rearrange("p t r -> p r t"),
+                out=wg[k][:, 2048 * q : 2048 * (q + 1)].rearrange("p (c i t) -> p c t i", i=4, t=4),
+                in_=planes[:].rearrange("p t (c i) -> p c t i", i=4),
             )
 
         def quant(k):

@@ -20,8 +20,9 @@ UNITS = 24
 ROPE_BANKS = 20
 PE_LAG = 4
 PAIR_LAG = 3
-S_SLOT = {21: 18, 23: 21}
+S_SLOT = {19: 15, 21: 18, 23: 21}
 S_UNITS = tuple(S_SLOT)
+SHARED_SIN = (9, 10)
 
 
 def tile_causalselfattention_pa_kernel(
@@ -302,17 +303,31 @@ def tile_causalselfattention_pa_kernel(
                 out=pairs(s_sb[p][:]), in0=pairs(u_sb[p][:])[:, :, ::-1], in1=pairs(sin_full[:]), op=MULT
             )
 
+        def sin_first_bank(p, k):
+            s_sb[p] = ring.tile([P, 1024], F32, name="s_sb", tag="wg%d" % ((k - 1) % 3), bufs=1, align_bytes=64)
+            nc.gpsimd.tensor_tensor(
+                out=pairs(half(s_sb[p], 0)),
+                in0=pairs(half(u_sb[p], 0))[:, :, ::-1],
+                in1=pairs(half(sin_full, 0)),
+                op=MULT,
+            )
+
         def rope_add(p, eng):
             o_sb = ring.tile([P, 1024], F32, name="o_sb", tag="o_sb", bufs=4)
             eng.tensor_tensor(out=o_sb[:], in0=a_sb[p][:], in1=s_sb[p][:], op=ADD)
             store_pair(p, o_sb[:])
 
+        def sin_bank(b):
+            p = b // 2
+            if p not in s_sb:
+                s_sb[p] = ring.tile([P, 1024], F32, name="s_v", tag="s_v", bufs=1)
+            nc.vector.tensor_tensor(
+                out=heads(half(s_sb[p], b)), in0=heads(acc[b][:])[:, :, :, ::-1], in1=table(sin2, b), op=MULT
+            )
+
         def rope_sin_on_vector(p):
-            s_sb[p] = ring.tile([P, 1024], F32, name="s_v", tag="s_v", bufs=1)
             for b in (2 * p, 2 * p + 1):
-                nc.vector.tensor_tensor(
-                    out=heads(half(s_sb[p], b)), in0=heads(acc[b][:])[:, :, :, ::-1], in1=table(sin2, b), op=MULT
-                )
+                sin_bank(b)
             o_last[p] = ring.tile([P, 1024], F32, name="o_sb", tag="o_sb", bufs=4)
 
         def rope_add_bank(b):
@@ -338,16 +353,22 @@ def tile_causalselfattention_pa_kernel(
                 scale_half(s, 0)
                 if 3 <= s <= 6:
                     x_quant(s - 3)
-                if s - 1 in S_UNITS:
+                if s - 1 in S_UNITS and k - 1 not in SHARED_SIN:
                     rope_add(p - 1, nc.vector)
                 if k >= 1:
                     quant(k - 1)
-                if p >= 0:
+                if k in SHARED_SIN:
+                    sin_first_bank(p, k)
+                    rope_cos(2 * p)
+                    rope_cos(2 * p + 1)
+                    sin_bank(2 * p + 1)
+                    rope_add(p, nc.gpsimd)
+                elif p >= 0:
                     rope_cos(2 * p)
                     rope_sin(p, k)
                 scale_half(s, 1)
             else:
-                if p >= 0:
+                if p >= 0 and k not in SHARED_SIN:
                     rope_cos(2 * p + 1)
                 if s not in S_UNITS:
                     if p >= 0:
@@ -379,7 +400,7 @@ def tile_causalselfattention_pa_kernel(
             for j in range(UNITS):
                 if j not in wb and (j <= s + lead or (j in S_UNITS and S_SLOT[j] == s + 1)):
                     cast(j)
-            if 0 <= b < ROPE_BANKS - 2:
+            if 0 <= b < ROPE_BANKS - 2 and not (b % 2 == 1 and b // 2 + PAIR_LAG in SHARED_SIN):
                 copy_u(b)
             for j in early:
                 scale_on_scalar(j)

@@ -18,6 +18,7 @@ ADD = mybir.AluOpType.add
 P = 128
 UNITS = 24
 ROPE_BANKS = 20
+G_CAST = (5,)
 PE_LAG = 4
 PAIR_LAG = 3
 S_SLOT = {19: 15, 21: 18, 23: 21}
@@ -156,6 +157,11 @@ def tile_causalselfattention_pa_kernel(
         def cast(j):
             wb[j] = ring.tile([P, 2048], BF16, name="wb", tag="wb", bufs=6)
             nc.scalar.copy(out=wb[j][:], in_=wq[j][:].rearrange("p a k -> p (a k)").bitcast(FP8))
+
+        def cast_on_gpsimd(j):
+            wb[j] = ring.tile([P, 2048], BF16, name="wbg", tag="wg0", bufs=1, align_bytes=64)
+            for a in range(4):
+                nc.gpsimd.tensor_copy(out=wb[j][:, 512 * a : 512 * (a + 1)], in_=wq[j][:, a, :].bitcast(FP8))
 
         def turn(words, bank, h):
             for a2 in range(2):
@@ -351,7 +357,9 @@ def tile_causalselfattention_pa_kernel(
             p = k - PAIR_LAG
             if s % 2 == 0:
                 scale_half(s, 0)
-                if 3 <= s <= 6:
+                if s == 4:
+                    x_quant(0)
+                if 4 <= s <= 6:
                     x_quant(s - 3)
                 if s - 1 in S_UNITS and k - 1 not in SHARED_SIN:
                     rope_add(p - 1, nc.vector)
@@ -374,8 +382,8 @@ def tile_causalselfattention_pa_kernel(
                     if p >= 0:
                         rope_add(p, nc.gpsimd)
                     scale_half(s, 0)
-                    if 3 <= s <= 6:
-                        x_quant(s - 3)
+                    if s == 5:
+                        x_quant(2)
                     scale_half(s, 1)
             x_banks = [(m, h) for m in range(4) for h in range(2) if m + 1 + h == s]
             for m, h in x_banks:
@@ -394,6 +402,9 @@ def tile_causalselfattention_pa_kernel(
                 for m in (2 * (s % 2), 2 * (s % 2) + 1):
                     new_bank(ROPE_BANKS + m, "acc" if m < 2 else "tp")
                     passes(ROPE_BANKS + m, (0, 1))
+            for j in G_CAST:
+                if s == 2 + G_CAST.index(j):
+                    cast_on_gpsimd(j)
             for m, h in x_banks:
                 x_out(m, h)
             lead = 2 if s < 4 else (3 if s < 8 else (4 if s < 12 else 5))

@@ -18,12 +18,12 @@ ADD = mybir.AluOpType.add
 P = 128
 UNITS = 24
 ROPE_BANKS = 20
-G_CAST = (5,)
+G_CAST = (5, 7)
 PE_LAG = 4
 PAIR_LAG = 3
-S_SLOT = {19: 15, 21: 18, 23: 21}
+S_SLOT = {17: 14, 19: 16, 21: 18, 23: 21}
 S_UNITS = tuple(S_SLOT)
-SHARED_SIN = (9, 10)
+SHARED_SIN = (8, 9, 10)
 
 
 def tile_causalselfattention_pa_kernel(
@@ -143,23 +143,23 @@ def tile_causalselfattention_pa_kernel(
         o_last = {}
 
         def cast0():
-            wb[0] = ring.tile([P, 2048], BF16, name="wb", tag="wb", bufs=6)
+            wb[0] = ring.tile([P, 2048], BF16, name="wb", tag="wb", bufs=8)
             for a in range(2):
                 nc.scalar.copy(out=wb[0][:, 512 * a : 512 * (a + 1)], in_=wq0[0][:, a, :].bitcast(FP8))
             nc.vector.tensor_copy(out=wb[0][:, 1024:2048], in_=wq0[1][:].rearrange("p a k -> p (a k)").bitcast(FP8))
 
         def cast1():
-            wb[1] = ring.tile([P, 2048], BF16, name="wb", tag="wb", bufs=6)
+            wb[1] = ring.tile([P, 2048], BF16, name="wb", tag="wb", bufs=8)
             flat = wq[1][:].rearrange("p a k -> p (a k)")
             nc.vector.tensor_copy(out=wb[1][:, 0:1024], in_=flat[:, 0:1024].bitcast(FP8))
             nc.scalar.copy(out=wb[1][:, 1024:2048], in_=flat[:, 1024:2048].bitcast(FP8))
 
         def cast(j):
-            wb[j] = ring.tile([P, 2048], BF16, name="wb", tag="wb", bufs=6)
+            wb[j] = ring.tile([P, 2048], BF16, name="wb", tag="wb", bufs=8)
             nc.scalar.copy(out=wb[j][:], in_=wq[j][:].rearrange("p a k -> p (a k)").bitcast(FP8))
 
         def cast_on_gpsimd(j):
-            wb[j] = ring.tile([P, 2048], BF16, name="wbg", tag="wg0", bufs=1, align_bytes=64)
+            wb[j] = ring.tile([P, 2048], BF16, name="wbg", tag="wg%d" % G_CAST.index(j), bufs=1, align_bytes=64)
             for a in range(4):
                 nc.gpsimd.tensor_copy(out=wb[j][:, 512 * a : 512 * (a + 1)], in_=wq[j][:, a, :].bitcast(FP8))
 
@@ -357,9 +357,8 @@ def tile_causalselfattention_pa_kernel(
             p = k - PAIR_LAG
             if s % 2 == 0:
                 scale_half(s, 0)
-                if s == 4:
-                    x_quant(0)
-                if 4 <= s <= 6:
+                if s in (4, 6):
+                    x_quant(s - 4)
                     x_quant(s - 3)
                 if s - 1 in S_UNITS and k - 1 not in SHARED_SIN:
                     rope_add(p - 1, nc.vector)
@@ -382,8 +381,6 @@ def tile_causalselfattention_pa_kernel(
                     if p >= 0:
                         rope_add(p, nc.gpsimd)
                     scale_half(s, 0)
-                    if s == 5:
-                        x_quant(2)
                     scale_half(s, 1)
             x_banks = [(m, h) for m in range(4) for h in range(2) if m + 1 + h == s]
             for m, h in x_banks:
@@ -403,11 +400,11 @@ def tile_causalselfattention_pa_kernel(
                     new_bank(ROPE_BANKS + m, "acc" if m < 2 else "tp")
                     passes(ROPE_BANKS + m, (0, 1))
             for j in G_CAST:
-                if s == 2 + G_CAST.index(j):
+                if s == 2 + 2 * G_CAST.index(j):
                     cast_on_gpsimd(j)
             for m, h in x_banks:
                 x_out(m, h)
-            lead = 2 if s < 4 else (3 if s < 8 else (4 if s < 12 else 5))
+            lead = 2 if s < 4 else (3 if s < 6 else (4 if s < 9 else (5 if s < 12 else 6)))
             for j in range(UNITS):
                 if j not in wb and (j <= s + lead or (j in S_UNITS and S_SLOT[j] == s + 1)):
                     cast(j)

@@ -19,6 +19,7 @@ P = 128
 UNITS = 24
 ROPE_BANKS = 20
 G_CAST = (5, 7)
+LONG_RUNS = 14
 PE_LAG = 4
 PAIR_LAG = 3
 S_SLOT = {17: 14, 19: 16, 21: 18, 23: 21}
@@ -390,8 +391,10 @@ def tile_causalselfattention_pa_kernel(
             for h in range(2):
                 if s + 1 < UNITS and s + 1 not in S_UNITS:
                     transposes(s + 1, h)
-                if b >= 0:
+                if b >= 0 and s < LONG_RUNS:
                     passes(b, (2 * h, 2 * h + 1))
+            if b >= 0 and s >= LONG_RUNS:
+                passes(b, range(4))
             early = [j for j in S_UNITS if S_SLOT[j] == s]
             for j in early:
                 transposes_by_u(j)

@@ -145,15 +145,15 @@ def tile_causalselfattention_pa_kernel(
 
         def cast0():
             wb[0] = ring.tile([P, 2048], BF16, name="wb", tag="wb", bufs=8)
-            for a in range(2):
-                nc.scalar.copy(out=wb[0][:, 512 * a : 512 * (a + 1)], in_=wq0[0][:, a, :].bitcast(FP8))
+            nc.scalar.copy(out=wb[0][:, 0:512], in_=wq0[0][:, 0, :].bitcast(FP8))
+            nc.vector.tensor_copy(out=wb[0][:, 512:1024], in_=wq0[0][:, 1, :].bitcast(FP8))
             nc.vector.tensor_copy(out=wb[0][:, 1024:2048], in_=wq0[1][:].rearrange("p a k -> p (a k)").bitcast(FP8))
 
         def cast1():
             wb[1] = ring.tile([P, 2048], BF16, name="wb", tag="wb", bufs=8)
             flat = wq[1][:].rearrange("p a k -> p (a k)")
-            nc.vector.tensor_copy(out=wb[1][:, 0:1024], in_=flat[:, 0:1024].bitcast(FP8))
-            nc.scalar.copy(out=wb[1][:, 1024:2048], in_=flat[:, 1024:2048].bitcast(FP8))
+            nc.vector.tensor_copy(out=wb[1][:, 0:512], in_=flat[:, 0:512].bitcast(FP8))
+            nc.scalar.copy(out=wb[1][:, 512:2048], in_=flat[:, 512:2048].bitcast(FP8))
 
         def cast(j):
             wb[j] = ring.tile([P, 2048], BF16, name="wb", tag="wb", bufs=8)
@@ -407,7 +407,7 @@ def tile_causalselfattention_pa_kernel(
                     cast_on_gpsimd(j)
             for m, h in x_banks:
                 x_out(m, h)
-            lead = 2 if s < 4 else (3 if s < 6 else (4 if s < 9 else (5 if s < 12 else 6)))
+            lead = 2 if s < 3 else (3 if s < 4 else (4 if s < 8 else (5 if s < 12 else 6)))
             for j in range(UNITS):
                 if j not in wb and (j <= s + lead or (j in S_UNITS and S_SLOT[j] == s + 1)):
                     cast(j)

@@ -24,7 +24,7 @@ PE_LAG = 4
 PAIR_LAG = 3
 S_SLOT = {17: 14, 19: 16, 21: 18, 23: 21}
 S_UNITS = tuple(S_SLOT)
-SHARED_SIN = (8, 9, 10)
+SHARED_SIN = (8, 9, 10, 11)
 
 
 def tile_causalselfattention_pa_kernel(
@@ -324,6 +324,11 @@ def tile_causalselfattention_pa_kernel(
             eng.tensor_tensor(out=o_sb[:], in0=a_sb[p][:], in1=s_sb[p][:], op=ADD)
             store_pair(p, o_sb[:])
 
+        def halves_add(p, th, eng):
+            if th == 0:
+                o_last[p] = ring.tile([P, 1024], F32, name="o_sb", tag="o_sb", bufs=4)
+            eng.tensor_tensor(out=half(o_last[p], th), in0=half(a_sb[p], th), in1=half(s_sb[p], th), op=ADD)
+
         def sin_bank(b):
             p = b // 2
             if p not in s_sb:
@@ -370,7 +375,10 @@ def tile_causalselfattention_pa_kernel(
                     rope_cos(2 * p)
                     rope_cos(2 * p + 1)
                     sin_bank(2 * p + 1)
-                    rope_add(p, nc.gpsimd)
+                    if k == UNITS // 2 - 1:
+                        halves_add(p, 0, nc.gpsimd)
+                    else:
+                        rope_add(p, nc.gpsimd)
                 elif p >= 0:
                     rope_cos(2 * p)
                     rope_sin(p, k)
@@ -417,7 +425,8 @@ def tile_causalselfattention_pa_kernel(
                 scale_on_scalar(j)
         last = ROPE_BANKS // 2 - 1
         rope_cos(2 * last)
-        rope_add(last - 1, nc.vector)
+        halves_add(last - 1, 1, nc.vector)
+        store_pair(last - 1, o_last[last - 1][:])
         quant(UNITS // 2 - 1)
         for m in range(4):
             passes(ROPE_BANKS + m, (2, 3))

@@ -19,7 +19,6 @@ P = 128
 UNITS = 24
 ROPE_BANKS = 20
 G_CAST = (5, 7)
-LONG_RUNS = 14
 PE_LAG = 4
 PAIR_LAG = 3
 S_SLOT = {17: 14, 19: 16, 21: 18, 23: 21}
@@ -399,9 +398,7 @@ def tile_causalselfattention_pa_kernel(
             for h in range(2):
                 if s + 1 < UNITS and s + 1 not in S_UNITS:
                     transposes(s + 1, h)
-                if b >= 0 and s < LONG_RUNS:
-                    passes(b, (2 * h, 2 * h + 1))
-            if b >= 0 and s >= LONG_RUNS:
+            if b >= 0:
                 passes(b, range(4))
             early = [j for j in S_UNITS if S_SLOT[j] == s]
             for j in early:

from contextlib import ExitStack

import concourse.mybir as mybir
from concourse.masks import make_identity

FLOPS = 2 * 512 * 2048 * 3072

F32 = mybir.dt.float32
BF16 = mybir.dt.bfloat16
U32 = mybir.dt.uint32
U8 = mybir.dt.uint8
FP8 = mybir.dt.float8_e4m3fn
FP8X4 = mybir.dt.float8_e4m3fn_x4
COPY = mybir.ActivationFunctionType.Copy
MULT = mybir.AluOpType.mult
ADD = mybir.AluOpType.add

P = 128
UNITS = 24
ROPE_BANKS = 20
G_CAST = (5, 7)
PE_LAG = 4
PAIR_LAG = 3
S_SLOT = {17: 14, 19: 16, 21: 18, 23: 21}
S_UNITS = tuple(S_SLOT)
SHARED_SIN = (8, 9, 10, 11)


def tile_causalselfattention_pa_kernel(
    tc, x, w_qkv_bytes, w_qkv_scale, freqs_cos, freqs_sin, out_0, out_1, out_2
):
    nc = tc.nc
    x_rows = x.flatten_outer_dims()
    out_rows = [
        out_0.rearrange("b t h d -> (b t) (h d)"),
        out_1.rearrange("b t h d -> (b t) (h d)"),
        out_2.rearrange("b t h d -> (b t) (h d)"),
    ]

    with ExitStack() as ctx:
        const = ctx.enter_context(tc.tile_pool(name="const", bufs=1))
        ring = ctx.enter_context(tc.tile_pool(name="ring", bufs=4))
        psum = ctx.enter_context(tc.psum_pool(name="psum", bufs=4))
        ctx.enter_context(tc.manual_schedule())

        scale_sb = const.tile([P, 16], F32, name="scale_sb")
        nc.scalar.dma_start(
            out=scale_sb[:].rearrange("p (g t) -> p g t", t=4),
            in_=w_qkv_scale.rearrange("o (g p t) -> p (o g) t", p=P, t=4),
        )
        cos_raw = const.tile([P, 2, 64], BF16, name="cos_raw")
        nc.scalar.dma_start(out=cos_raw[:], in_=freqs_cos.rearrange("(th p) j -> p th j", p=P))
        sin_raw = const.tile([P, 2, 64], BF16, name="sin_raw")
        nc.scalar.dma_start(out=sin_raw[:], in_=freqs_sin.rearrange("(th p) j -> p th j", p=P))

        warm_in = const.tile([P, 1], F32, name="warm_in")
        warm_out = const.tile([P, 1], F32, name="warm_out")
        nc.gpsimd.memset(warm_in[:], 0.0)
        nc.scalar.copy(out=warm_out[:], in_=warm_in[:])

        ident = const.tile([P, P], F32, name="ident")
        make_identity(nc, ident[:])

        wq = {}
        wq0 = {}
        xs = {}

        def load_w0(h):
            wq0[h] = const.tile([P, 2, 512], U8, name="wq0_%d" % h)
            nc.sync.dma_start(
                out=wq0[h][:], in_=w_qkv_bytes[256 * h : 256 * (h + 1), 0:512].rearrange("(a p) k -> p a k", p=P)
            )

        def load_w(j):
            i, g = j // 4, j % 4
            wq[j] = const.tile([P, 4, 512], U8, name="wq%d" % j)
            nc.sync.dma_start(
                out=wq[j][:],
                in_=w_qkv_bytes[512 * i : 512 * (i + 1), 512 * g : 512 * (g + 1)].rearrange(
                    "(a p) k -> p a k", p=P
                ),
            )

        def load_x(m):
            xs[m] = const.tile([P, 2048], BF16, name="xs%d" % m)
            nc.sync.dma_start(out=xs[m][:], in_=x_rows[128 * m : 128 * (m + 1), :])

        load_w0(0)
        load_w0(1)
        load_w(1)
        load_w(2)
        for m in range(4):
            load_x(m)
            load_w(m + 3)
        for j in range(7, UNITS):
            load_w(j)

        cos2 = const.tile([P, 2, 64, 2], F32, name="cos2")
        sin2 = const.tile([P, 2, 64, 2], F32, name="sin2")
        sin_full = const.tile([P, 1024], F32, name="sin_full")
        sign = const.tile([P, 2], F32, name="sign")

        def tables():
            nc.vector.memset(sign[:, 0:1], -1.0)
            nc.vector.memset(sign[:, 1:2], 1.0)
            nc.gpsimd.tensor_tensor(
                out=sin2[:].rearrange("p t j e -> p (t j) e"),
                in0=sin_raw[:].rearrange("p t j -> p (t j)").unsqueeze(2).to_broadcast([P, 128, 2]),
                in1=sign[:].unsqueeze(1).to_broadcast([P, 128, 2]),
                op=MULT,
            )
            nc.gpsimd.tensor_scalar(
                out=cos2[:].rearrange("p t j e -> p (t j) e"),
                in0=cos_raw[:].rearrange("p t j -> p (t j)").unsqueeze(2).to_broadcast([P, 128, 2]),
                scalar1=1.0,
                scalar2=0.0,
                op0=MULT,
                op1=ADD,
            )
            nc.gpsimd.tensor_scalar(
                out=sin_full[:].rearrange("p (t h n) -> p t h n", t=2, h=4),
                in0=sin2[:].rearrange("p t j e -> p t (j e)").unsqueeze(2).to_broadcast([P, 2, 4, 128]),
                scalar1=1.0,
                scalar2=0.0,
                op0=MULT,
                op1=ADD,
            )

        xg = [const.tile([P, 2048], BF16, name="xg%d" % m, align_bytes=64) for m in range(4)]
        xc = [const.tile([P, 512], U32, name="xc%d" % m, align_bytes=64) for m in range(4)]
        xsc = [const.tile([P, 512], U8, name="xsc%d" % m, align_bytes=64) for m in range(4)]

        wb = {}
        tp = {}
        xt = {}
        wg = {}
        wc = {}
        ws = {}
        acc = {}
        u_sb = {}
        a_sb = {}
        s_sb = {}
        o_last = {}

        def cast0():
            wb[0] = ring.tile([P, 2048], BF16, name="wb", tag="wb", bufs=8)
            nc.scalar.copy(out=wb[0][:, 0:512], in_=wq0[0][:, 0, :].bitcast(FP8))
            nc.vector.tensor_copy(out=wb[0][:, 512:1024], in_=wq0[0][:, 1, :].bitcast(FP8))
            nc.vector.tensor_copy(out=wb[0][:, 1024:2048], in_=wq0[1][:].rearrange("p a k -> p (a k)").bitcast(FP8))

        def cast1():
            wb[1] = ring.tile([P, 2048], BF16, name="wb", tag="wb", bufs=8)
            flat = wq[1][:].rearrange("p a k -> p (a k)")
            nc.vector.tensor_copy(out=wb[1][:, 0:512], in_=flat[:, 0:512].bitcast(FP8))
            nc.scalar.copy(out=wb[1][:, 512:2048], in_=flat[:, 512:2048].bitcast(FP8))

        def cast(j):
            wb[j] = ring.tile([P, 2048], BF16, name="wb", tag="wb", bufs=8)
            nc.scalar.copy(out=wb[j][:], in_=wq[j][:].rearrange("p a k -> p (a k)").bitcast(FP8))

        def cast_on_gpsimd(j):
            wb[j] = ring.tile([P, 2048], BF16, name="wbg", tag="wg%d" % G_CAST.index(j), bufs=1, align_bytes=64)
            for a in range(4):
                nc.gpsimd.tensor_copy(out=wb[j][:, 512 * a : 512 * (a + 1)], in_=wq[j][:, a, :].bitcast(FP8))

        def turn(words, bank, h):
            for a2 in range(2):
                for u in range(2):
                    a = 2 * h + a2
                    nc.tensor.transpose(
                        bank[:, u, 128 * a2 : 128 * (a2 + 1)],
                        words[:, 256 * a + u : 256 * (a + 1) : 2],
                        ident[:],
                    )

        def transposes(j, h):
            tp[(j, h)] = psum.tile([P, 2, 256], F32, name="tp", tag="tp")
            turn(wb[j][:].bitcast(F32), tp[(j, h)], h)

        def transposes_by_u(j):
            words = wb[j][:].bitcast(F32)
            for u in range(2):
                tp[(j, u)] = psum.tile([P, 2, 256], F32, name="tp", tag="tp")
                for a in range(4):
                    nc.tensor.transpose(
                        tp[(j, u)][:].rearrange("p u r -> p (u r)")[:, 128 * a : 128 * (a + 1)],
                        words[:, 256 * a + u : 256 * (a + 1) : 2],
                        ident[:],
                    )

        def x_transposes(m, h):
            words = xs[m][:].bitcast(F32)
            xt[(m, h)] = psum.tile([P, 2, 2, 128], F32, name="xt", tag="acc")
            for g2 in range(2):
                g = 2 * h + g2
                for u in range(2):
                    nc.tensor.transpose(xt[(m, h)][:, g2, u, :], words[:, 256 * g + u : 256 * (g + 1) : 2], ident[:])

        def x_out(m, h):
            nc.scalar.copy(
                out=xg[m][:, 1024 * h : 1024 * (h + 1)].bitcast(F32).rearrange("p (g r u) -> p g r u", g=2, u=2),
                in_=xt[(m, h)][:].rearrange("p g u r -> p g r u"),
            )

        def x_quant(m):
            nc.vector.quantize_mx(out=xc[m][:].bitcast(FP8X4), scales=xsc[m][:], in_=xg[m][:])

        def scale_half(j, h):
            g = j % 4
            k, q = j // 2, j % 2
            if k not in wg:
                wg[k] = ring.tile([P, 4096], BF16, name="wg", tag="wg%d" % (k % 3), bufs=1, align_bytes=64)
            c0 = 2048 * q + 1024 * h
            nc.vector.tensor_tensor(
                out=wg[k][:, c0 : c0 + 1024].rearrange("p (r u e) -> p r u e", u=2, e=2),
                in0=tp[(j, h)][:]
                .rearrange("p u r -> p (u r)")
                .bitcast(BF16)
                .rearrange("p (u r e) -> p r u e", u=2, e=2),
                in1=scale_sb[:, 4 * g : 4 * g + 4]
                .rearrange("p (o u e) -> p o u e", o=1, u=2, e=2)
                .to_broadcast([P, 256, 2, 2]),
                op=MULT,
            )

        def scale_on_scalar(j):
            g = j % 4
            k, q = j // 2, j % 2
            if k not in wg:
                wg[k] = ring.tile([P, 4096], BF16, name="wg", tag="wg%d" % (k % 3), bufs=1, align_bytes=64)
            planes = ring.tile([P, 4, 512], BF16, name="planes", tag="planes", bufs=1)
            for u in range(2):
                bank = tp[(j, u)][:].rearrange("p u r -> p (u r)").bitcast(BF16).rearrange("p (r e) -> p e r", e=2)
                for e in range(2):
                    t = 2 * u + e
                    nc.scalar.activation(
                        out=planes[:, t, :], in_=bank[:, e, :], func=COPY, scale=scale_sb[:, 4 * g + t : 4 * g + t + 1]
                    )
            nc.scalar.copy(
                out=wg[k][:, 2048 * q : 2048 * (q + 1)].rearrange("p (c i t) -> p c t i", i=4, t=4),
                in_=planes[:].rearrange("p t (c i) -> p c t i", i=4),
            )

        def quant(k):
            wc[k] = ring.tile([P, 1024], U32, name="wc", tag="wc", bufs=4, align_bytes=64)
            ws[k] = ring.tile([P, 1024], U8, name="ws", tag="ws", bufs=4, align_bytes=64)
            nc.vector.quantize_mx(out=wc[k][:].bitcast(FP8X4), scales=ws[k][:], in_=wg[k][:])

        def new_bank(b, tag):
            acc[b] = psum.tile([P, 512], F32, name="acc", tag=tag)

        def passes(b, gs):
            i, m = b // 4, b % 4
            for g in gs:
                j = 4 * i + g
                cols = slice(512 * (j % 2), 512 * (j % 2 + 1))
                nc.tensor.matmul_mx(
                    out=acc[b][:],
                    lhsT=xc[m][:, 128 * g : 128 * (g + 1)].bitcast(FP8X4),
                    lhsT_scale=xsc[m][:, 128 * g : 128 * (g + 1)],
                    rhs=wc[j // 2][:, cols].bitcast(FP8X4),
                    rhs_scale=ws[j // 2][:, cols],
                    start=(g == 0),
                    stop=(g == 3),
                )

        def out_view(b):
            i = b // 4
            dst = out_rows[0] if i < 4 else out_rows[i - 3]
            c0 = 512 * i if i < 4 else 0
            return dst[:, c0 : c0 + 512]

        def store(b, tile_ap):
            m = b % 4
            nc.sync.dma_start(out=out_view(b)[128 * m : 128 * (m + 1), :], in_=tile_ap)

        def store_pair(p, tile_ap):
            m = (2 * p) % 4
            nc.sync.dma_start(
                out=out_view(2 * p)[128 * m : 128 * (m + 2), :].rearrange("(t p) c -> p t c", p=P),
                in_=tile_ap.rearrange("p (t c) -> p t c", t=2),
            )

        def heads(ap):
            return ap.rearrange("p (h j e) -> p h j e", h=4, e=2)

        def pairs(ap):
            return ap.rearrange("p (n e) -> p n e", e=2)

        def table(t, b):
            return t[:, b % 2, :, :].unsqueeze(1).to_broadcast([P, 4, 64, 2])

        def half(t, b):
            return t[:, 512 * (b % 2) : 512 * (b % 2 + 1)]

        def copy_u(b):
            if b % 2 == 0:
                u_sb[b // 2] = ring.tile([P, 1024], F32, name="u_sb", tag="u_sb", bufs=3)
            nc.scalar.copy(out=half(u_sb[b // 2], b), in_=acc[b][:])

        def rope_cos(b):
            if b % 2 == 0:
                a_sb[b // 2] = ring.tile([P, 1024], F32, name="a_sb", tag="a_sb", bufs=3)
            nc.vector.tensor_tensor(out=heads(half(a_sb[b // 2], b)), in0=heads(acc[b][:]), in1=table(cos2, b), op=MULT)

        def rope_sin(p, k):
            s_sb[p] = ring.tile([P, 1024], F32, name="s_sb", tag="wg%d" % ((k - 1) % 3), bufs=1, align_bytes=64)
            nc.gpsimd.tensor_tensor(
                out=pairs(s_sb[p][:]), in0=pairs(u_sb[p][:])[:, :, ::-1], in1=pairs(sin_full[:]), op=MULT
            )

        def sin_first_bank(p, k):
            s_sb[p] = ring.tile([P, 1024], F32, name="s_sb", tag="wg%d" % ((k - 1) % 3), bufs=1, align_bytes=64)
            nc.gpsimd.tensor_tensor(
                out=pairs(half(s_sb[p], 0)),
                in0=pairs(half(u_sb[p], 0))[:, :, ::-1],
                in1=pairs(half(sin_full, 0)),
                op=MULT,
            )

        def rope_add(p, eng):
            o_sb = ring.tile([P, 1024], F32, name="o_sb", tag="o_sb", bufs=4)
            eng.tensor_tensor(out=o_sb[:], in0=a_sb[p][:], in1=s_sb[p][:], op=ADD)
            store_pair(p, o_sb[:])

        def halves_add(p, th, eng):
            if th == 0:
                o_last[p] = ring.tile([P, 1024], F32, name="o_sb", tag="o_sb", bufs=4)
            eng.tensor_tensor(out=half(o_last[p], th), in0=half(a_sb[p], th), in1=half(s_sb[p], th), op=ADD)

        def sin_bank(b):
            p = b // 2
            if p not in s_sb:
                s_sb[p] = ring.tile([P, 1024], F32, name="s_v", tag="s_v", bufs=1)
            nc.vector.tensor_tensor(
                out=heads(half(s_sb[p], b)), in0=heads(acc[b][:])[:, :, :, ::-1], in1=table(sin2, b), op=MULT
            )

        def rope_sin_on_vector(p):
            for b in (2 * p, 2 * p + 1):
                sin_bank(b)
            o_last[p] = ring.tile([P, 1024], F32, name="o_sb", tag="o_sb", bufs=4)

        def rope_add_bank(b):
            p = b // 2
            nc.vector.tensor_tensor(out=half(o_last[p], b), in0=half(a_sb[p], b), in1=half(s_sb[p], b), op=ADD)
            store(b, half(o_last[p], b))

        def plain_out(b):
            v_sb = ring.tile([P, 512], F32, name="v_sb", tag="v_sb", bufs=4)
            nc.scalar.copy(out=v_sb[:], in_=acc[b][:])
            store(b, v_sb[:])

        cast0()
        cast1()
        tables()
        transposes(0, 0)
        transposes(0, 1)
        for s in range(UNITS):
            k = s // 2
            b = s - PE_LAG
            p = k - PAIR_LAG
            if s % 2 == 0:
                scale_half(s, 0)
                if s in (4, 6):
                    x_quant(s - 4)
                    x_quant(s - 3)
                if s - 1 in S_UNITS and k - 1 not in SHARED_SIN:
                    rope_add(p - 1, nc.vector)
                if k >= 1:
                    quant(k - 1)
                if k in SHARED_SIN:
                    sin_first_bank(p, k)
                    rope_cos(2 * p)
                    rope_cos(2 * p + 1)
                    sin_bank(2 * p + 1)
                    if k == UNITS // 2 - 1:
                        halves_add(p, 0, nc.gpsimd)
                    else:
                        rope_add(p, nc.gpsimd)
                elif p >= 0:
                    rope_cos(2 * p)
                    rope_sin(p, k)
                scale_half(s, 1)
            else:
                if p >= 0 and k not in SHARED_SIN:
                    rope_cos(2 * p + 1)
                if s not in S_UNITS:
                    if p >= 0:
                        rope_add(p, nc.gpsimd)
                    scale_half(s, 0)
                    scale_half(s, 1)
            x_banks = [(m, h) for m in range(4) for h in range(2) if m + 1 + h == s]
            for m, h in x_banks:
                x_transposes(m, h)
            if b >= 0:
                new_bank(b, "acc")
            for h in range(2):
                if s + 1 < UNITS and s + 1 not in S_UNITS:
                    transposes(s + 1, h)
            if b >= 0:
                passes(b, range(4))
            early = [j for j in S_UNITS if S_SLOT[j] == s]
            for j in early:
                transposes_by_u(j)
            if s >= UNITS - 2:
                for m in (2 * (s % 2), 2 * (s % 2) + 1):
                    new_bank(ROPE_BANKS + m, "acc" if m < 2 else "tp")
                    passes(ROPE_BANKS + m, (0, 1))
            for j in G_CAST:
                if s == 2 + 2 * G_CAST.index(j):
                    cast_on_gpsimd(j)
            for m, h in x_banks:
                x_out(m, h)
            lead = 2 if s < 3 else (3 if s < 4 else (4 if s < 8 else (5 if s < 12 else 6)))
            for j in range(UNITS):
                if j not in wb and (j <= s + lead or (j in S_UNITS and S_SLOT[j] == s + 1)):
                    cast(j)
            if 0 <= b < ROPE_BANKS - 2 and not (b % 2 == 1 and b // 2 + PAIR_LAG in SHARED_SIN):
                copy_u(b)
            for j in early:
                scale_on_scalar(j)
        last = ROPE_BANKS // 2 - 1
        rope_cos(2 * last)
        halves_add(last - 1, 1, nc.vector)
        store_pair(last - 1, o_last[last - 1][:])
        quant(UNITS // 2 - 1)
        for m in range(4):
            passes(ROPE_BANKS + m, (2, 3))
        rope_cos(2 * last + 1)
        rope_sin_on_vector(last)
        plain_out(ROPE_BANKS)
        plain_out(ROPE_BANKS + 1)
        rope_add_bank(2 * last)
        plain_out(ROPE_BANKS + 2)
        rope_add_bank(2 * last + 1)
        plain_out(ROPE_BANKS + 3)
